import numpy as np
import ml_dtypes


def mxq(x, axis, fmt="e4m3"):
    dtype, down = {"e4m3": (ml_dtypes.float8_e4m3fn, 7), "e5m2": (ml_dtypes.float8_e5m2, 14)}[fmt]
    v = np.moveaxis(np.asarray(x, np.float32).astype(ml_dtypes.bfloat16).astype(np.float64), axis, -1)
    blocks = v.reshape(v.shape[:-1] + (-1, 32))
    amax = np.abs(blocks).max(-1, keepdims=True)
    byte = np.maximum(np.where(amax > 0, np.frexp(amax)[1] - 1 + 127, 0) - down, 1)
    scale = np.exp2(byte - 127.0)
    codes = (blocks / scale).astype(np.float32).astype(dtype).astype(np.float64)
    return np.moveaxis((codes * scale).reshape(v.shape), -1, axis)


WIDE = False


def mx_kscale(k):
    if not WIDE:
        return np.ones(k)
    levels = np.array([20, -20, 10, -10, 0])
    a = np.random.permutation(np.resize(levels, k // 512 * 4)).reshape(k // 512, 4)
    idx = np.arange(k)
    return np.exp2(a[idx // 512, idx % 128 // 32])


BF16 = ml_dtypes.bfloat16


def bf(x):
    return np.asarray(x, np.float32).astype(BF16)


def f64(x):
    return np.asarray(x).astype(np.float64)


B, H, W, C, U, K = 8, 18, 18, 512, 512, 3
OY, OX = H - K + 1, W - K + 1
T = B * OY * OX
D = K * K * C
P_SCALE = 5.0
Q_SCALE = 0.3
EPS = 1e-6
L2_EPS = 1e-12


def im2col_valid(x, k):
    nb, nh, nw, nc_ = x.shape
    oy, ox = nh - k + 1, nw - k + 1
    patches = np.stack([x[:, i:i + oy, j:j + ox, :] for i in range(k) for j in range(k)], axis=3)
    return patches.reshape(nb, oy * ox, k * k * nc_), oy, ox


def image_scale():
    blk = np.sort(mx_kscale(T)[::32])
    pick = (np.arange(B) * (len(blk) - 1)) // (B - 1)
    v = blk[pick]
    sb = np.empty(B)
    sb[0::2] = v[:B // 2]
    sb[1::2] = v[::-1][:B // 2]
    return sb


def cos_parts(x, w, q):
    x, w, q = f64(x), f64(w), f64(q)
    nb = x.shape[0]
    patches, oy, ox = im2col_valid(x, K)
    qq = np.square(q / Q_SCALE)
    x_norm = np.sqrt(np.maximum(np.sum(np.square(patches), axis=2, keepdims=True), L2_EPS)) + qq
    w_norm = np.sqrt(np.maximum(np.sum(np.square(w), axis=1, keepdims=True), L2_EPS)) + qq
    sim = (patches / x_norm) @ (w / w_norm)
    return (1.0 / x_norm).reshape(nb, oy, ox), sim.reshape(nb, oy, ox, w.shape[2])


def setup_inputs():
    sb = image_scale()[:, None, None, None]
    g = np.random.uniform(0.5, 1.5, (1, 1, U)) * np.sign(np.random.standard_normal((1, 1, U)))
    x0 = bf(np.abs(np.random.standard_normal((B, H, W, C))) * 0.25)
    w = bf((np.random.standard_normal((1, D, U)) + g) * 2.0 / np.sqrt(D))
    p = bf(0.7 * P_SCALE * (1.0 + 0.1 * np.random.standard_normal(U)))
    q = bf(0.2 * (1.0 + 0.1 * np.random.standard_normal(1)))
    go = bf(np.random.standard_normal((B, OY, OX, U)) * np.exp2(np.random.randint(-12, 1, (B, OY, OX, 1))) * 32.0 / sb)
    rn, sim = cos_parts(x0, w, q)
    return {"x": bf(f64(x0) * sb), "w": w, "p": p, "q": q,
            "x_rnorm": np.asarray(rn, np.float32), "sim": np.asarray(sim, np.float32), "grad_out": go}


def reference(x, w, p, q, x_rnorm, sim, grad_out):
    x, w, p, q = f64(x), f64(w), f64(p), f64(q)
    patches, oy, ox = im2col_valid(x, K)
    xn = patches.reshape(T, D) * f64(x_rnorm).reshape(T, 1)
    pp = np.square(p / P_SCALE)
    sm = f64(sim).reshape(T, U)
    dsim = f64(grad_out).reshape(T, U) * pp * np.power(np.abs(sm) + EPS, pp - 1.0)
    dwn = mxq(xn, 0, "e4m3").T @ mxq(dsim, 0, "e5m2")
    w2 = w[0]
    qq = np.square(q / Q_SCALE)
    r = np.sqrt(np.maximum(np.sum(np.square(w2), axis=0), L2_EPS))
    w_norm = r + qq
    c = np.sum(dwn * w2, axis=0)
    gw = dwn / w_norm - w2 * (c / (np.square(w_norm) * r))
    return gw[None]

@@ -1,0 +1,293 @@
+import concourse.mybir as mybir
+from concourse.masks import make_identity
+
+F32 = mybir.dt.float32
+BF16 = mybir.dt.bfloat16
+U32 = mybir.dt.uint32
+U8 = mybir.dt.uint8
+E4M3_X4 = mybir.dt.float8_e4m3fn_x4
+E5M2_X4 = mybir.dt.float8_e5m2_x4
+ACT = mybir.ActivationFunctionType
+ALU = mybir.AluOpType
+
+P = 128
+PACK = 4
+B, H, W, C = 8, 18, 18, 512
+KS = 3
+OY, OX = H - KS + 1, W - KS + 1
+U = 512
+D = KS * KS * C
+SHIFTS = KS * KS
+PASSES = OX // PACK
+U_TILES = U // P
+D_TILES_PER_SHIFT = C // P
+P_SCALE, Q_SCALE, EPS, L2_EPS = 5.0, 0.3, 1e-6, 1e-12
+
+LEAD = 3
+
+FLOPS = 2 * B * OY * OX * D * U
+
+
+def tile_cossim2d_v_kernel(tc, x, w, p, q, x_rnorm, sim, grad_out, out):
+    nc = tc.nc
+    sim_rows = sim.rearrange("b y z u -> (b y) z u")
+    go_rows = grad_out.rearrange("b y z u -> (b y) z u")
+    w_tiles = w.rearrange("o (t p) u -> p (o t) u", p=P)
+    out_tiles = out.rearrange("o (t p) u -> p (o t) u", p=P)
+
+    def u_cols(ub):
+        return slice(ub * P, (ub + 1) * P)
+
+    def d_cols(s):
+        return slice(s * C, (s + 1) * C)
+
+    def z_cols(g):
+        return slice(g * PACK, (g + 1) * PACK)
+
+    with (
+        tc.manual_schedule(),
+        tc.tile_pool(name="const", bufs=1) as const,
+        tc.tile_pool(name="keep", bufs=1) as keep,
+        tc.tile_pool(name="x_pool", bufs=2) as x_pool,
+        tc.tile_pool(name="xn_pool", bufs=4) as xn_pool,
+        tc.tile_pool(name="code_pool", bufs=LEAD + 1) as code_pool,
+    ):
+        x_rows = {}
+
+        def load_x_rows(i, images, queue):
+            if i not in x_rows:
+                x_rows[i] = x_pool.tile([P, W, C], BF16, name="x_rows")
+            for b in images:
+                queue.dma_start(out=x_rows[i][b * OY : (b + 1) * OY, :, :], in_=x[b, i : i + OY, :, :])
+
+        even_images = range(0, B, 2)
+        odd_images = range(1, B, 2)
+
+        rnorm = const.tile([P, OX], F32)
+        nc.sync.dma_start(out=rnorm[:], in_=x_rnorm.rearrange("b y z -> (b y) z"))
+        load_x_rows(0, even_images, nc.sync)
+        load_x_rows(0, odd_images, nc.scalar)
+
+        p_rows = const.tile([P, P], BF16)
+        nc.vector.memset(p_rows[:], 0.0)
+        nc.scalar.dma_start(out=p_rows[0:U_TILES, :], in_=p.rearrange("(r c) -> r c", c=P))
+        q_col = const.tile([P, 1], BF16)
+        nc.scalar.dma_start(out=q_col[:], in_=q.partition_broadcast(P))
+
+        ident_bf16 = const.tile([P, P], BF16)
+        make_identity(nc, ident_bf16[:])
+        ident_f32 = const.tile([P, P], F32)
+        make_identity(nc, ident_f32[:])
+
+        w_t = keep.tile([P, U_TILES, D], BF16)
+        d_codes = keep.tile([P, PASSES, U], U32, align_bytes=64)
+        d_scales = keep.tile([P, PASSES, U], U8, align_bytes=64)
+
+        xn_codes = {}
+        xn_scales = {}
+
+        def prepare_xn(s):
+            i, j = divmod(s, KS)
+            xn_codes[s] = code_pool.tile([P, PASSES, C], U32, name="xn_codes", align_bytes=64)
+            xn_scales[s] = code_pool.tile([P, PASSES, C], U8, name="xn_scales", align_bytes=64)
+            grouped = {}
+            for g in range(PASSES):
+                planes = xn_pool.tile([P, PACK, C], BF16, name="planes", bufs=3)
+                for t in range(PACK):
+                    z = g * PACK + t
+                    nc.vector.tensor_scalar_mul(
+                        out=planes[:, t, :], in0=x_rows[i][:, z + j, :], scalar1=rnorm[:, z : z + 1]
+                    )
+                grouped[g] = xn_pool.tile([P, C, PACK], BF16, name="grouped", align_bytes=64)
+                copier = nc.scalar.copy if (s > LEAD and g % 2 == 0) else nc.vector.tensor_copy
+                copier(
+                    out=grouped[g][:].rearrange("p (c r) t -> p c t r", r=4),
+                    in_=planes[:].rearrange("p t (c r) -> p c t r", r=4),
+                )
+            for g in range(PASSES):
+                nc.vector.quantize_mx(
+                    out=xn_codes[s][:, g, :].bitcast(E4M3_X4),
+                    scales=xn_scales[s][:, g, :],
+                    in_=grouped[g][:].rearrange("p c t -> p (c t)"),
+                )
+
+        a_col = const.tile([P, U_TILES], F32)
+        neg_a_over_r = const.tile([P, U_TILES], F32)
+
+        with (
+            tc.tile_pool(name="early", bufs=2) as early,
+            tc.psum_pool(name="early_psum", bufs=4) as early_psum,
+        ):
+            go_sb = early.tile([P, OX, U], BF16, bufs=1)
+            power = early.tile([P, U_TILES, OX, P], F32, bufs=1)
+
+            p_ps = early_psum.tile([P, P], BF16, tag="turn")
+            nc.tensor.transpose(p_ps[:], p_rows[:], ident_bf16[:])
+            e_col = const.tile([P, U_TILES], F32)
+            nc.scalar.activation(out=e_col[:], in_=p_ps[:, 0:U_TILES], func=ACT.Square, scale=1.0 / P_SCALE)
+            e_minus_1 = const.tile([P, U_TILES], F32)
+            nc.gpsimd.tensor_scalar_add(out=e_minus_1[:], in0=e_col[:], scalar1=-1.0)
+            qq_col = const.tile([P, 1], F32)
+            nc.scalar.activation(out=qq_col[:], in_=q_col[:], func=ACT.Square, scale=1.0 / Q_SCALE)
+
+            for g in range(PASSES):
+                sim_sb = early.tile([P, PACK, U], F32)
+                nc.sync.dma_start(out=sim_sb[:], in_=sim_rows[:, z_cols(g), :])
+                for ub in range(U_TILES):
+                    sim_t = early_psum.tile([P, PACK, P], F32, tag="turn")
+                    for t in range(PACK):
+                        nc.tensor.transpose(sim_t[:, t, :], sim_sb[:, t, u_cols(ub)], ident_f32[:])
+                    nc.scalar.activation(out=power[:, ub, z_cols(g), :], in_=sim_t[:], func=ACT.Abs)
+            nc.sync.dma_start(out=go_sb[:], in_=go_rows)
+            load_x_rows(1, odd_images, nc.scalar)
+
+            r2_ps = [
+                early_psum.tile([P, P], F32, name="r2_ps%d" % ub, bufs=1) for ub in range(U_TILES)
+            ]
+            for s in range(SHIFTS):
+                w_sb = early.tile([P, D_TILES_PER_SHIFT, U], BF16, name="w_sb", bufs=3)
+                nc.sync.dma_start(
+                    out=w_sb[:], in_=w_tiles[:, s * D_TILES_PER_SHIFT : (s + 1) * D_TILES_PER_SHIFT, :]
+                )
+                for ub in range(U_TILES):
+                    for t in range(D_TILES_PER_SHIFT):
+                        nc.tensor.matmul(
+                            out=r2_ps[ub][:],
+                            lhsT=w_sb[:, t, u_cols(ub)],
+                            rhs=w_sb[:, t, u_cols(ub)],
+                            start=(s == 0 and t == 0),
+                            stop=(s == SHIFTS - 1 and t == D_TILES_PER_SHIFT - 1),
+                        )
+            load_x_rows(1, even_images, nc.sync)
+
+            for s in range(LEAD):
+                prepare_xn(s)
+
+            r2_col = const.tile([P, U_TILES], F32)
+            for ub in range(U_TILES):
+                off_diagonal_zeroed = early.tile([P, P], F32)
+                nc.vector.scalar_tensor_tensor(
+                    out=off_diagonal_zeroed[:],
+                    in0=r2_ps[ub][:],
+                    scalar=1.0,
+                    in1=ident_f32[:],
+                    op0=ALU.mult,
+                    op1=ALU.mult,
+                    accum_out=r2_col[:, ub : ub + 1],
+                )
+            nc.vector.tensor_scalar_max(out=r2_col[:], in0=r2_col[:], scalar1=L2_EPS)
+
+            ln_e = const.tile([P, U_TILES], F32)
+            nc.scalar.activation(out=ln_e[:], in_=e_col[:], func=ACT.Ln)
+            for ub in range(U_TILES):
+                nc.scalar.activation(out=power[:, ub], in_=power[:, ub], func=ACT.Ln, bias=EPS)
+
+            for g in range(PASSES):
+                d_grouped = xn_pool.tile([P, U, PACK], BF16, name="grouped", align_bytes=64)
+                for ub in range(U_TILES):
+                    nc.scalar.activation(
+                        out=power[:, ub, z_cols(g), :],
+                        in_=power[:, ub, z_cols(g), :],
+                        func=ACT.Exp,
+                        scale=e_minus_1[:, ub : ub + 1],
+                        bias=ln_e[:, ub : ub + 1],
+                    )
+                    power_rows = early_psum.tile([P, PACK, P], F32, tag="turn")
+                    for t in range(PACK):
+                        nc.tensor.transpose(power_rows[:, t, :], power[:, ub, g * PACK + t, :], ident_f32[:])
+                    nc.vector.tensor_tensor(
+                        out=d_grouped[:, u_cols(ub), :],
+                        in0=power_rows[:].rearrange("p t u -> p u t"),
+                        in1=go_sb[:, z_cols(g), u_cols(ub)].rearrange("p t u -> p u t"),
+                        op=ALU.mult,
+                    )
+                nc.vector.quantize_mx(
+                    out=d_codes[:, g, :].bitcast(E5M2_X4),
+                    scales=d_scales[:, g, :],
+                    in_=d_grouped[:].rearrange("p u t -> p (u t)"),
+                )
+
+            r_col = const.tile([P, U_TILES], F32)
+            nc.scalar.activation(out=r_col[:], in_=r2_col[:], func=ACT.Sqrt)
+            w_norm = const.tile([P, U_TILES], F32)
+            nc.vector.tensor_scalar_add(out=w_norm[:], in0=r_col[:], scalar1=qq_col[:, 0:1])
+            nc.vector.reciprocal(out=a_col[:], in_=w_norm[:])
+            nc.vector.tensor_mul(out=w_norm[:], in0=w_norm[:], in1=r_col[:])
+            nc.vector.reciprocal(out=neg_a_over_r[:], in_=w_norm[:])
+            nc.vector.tensor_scalar_mul(out=neg_a_over_r[:], in0=neg_a_over_r[:], scalar1=-1.0)
+
+            for s in range(SHIFTS):
+                w_sb = early.tile([P, D_TILES_PER_SHIFT, U], BF16, name="w_sb", bufs=3)
+                nc.sync.dma_start(
+                    out=w_sb[:], in_=w_tiles[:, s * D_TILES_PER_SHIFT : (s + 1) * D_TILES_PER_SHIFT, :]
+                )
+                for ub in range(U_TILES):
+                    w_turn = early_psum.tile([P, D_TILES_PER_SHIFT, P], BF16, tag="turn")
+                    for t in range(D_TILES_PER_SHIFT):
+                        nc.tensor.transpose(w_turn[:, t, :], w_sb[:, t, u_cols(ub)], ident_bf16[:])
+                    nc.scalar.copy(
+                        out=w_t[:, ub, d_cols(s)].rearrange("p (t d) -> p t d", d=P), in_=w_turn[:]
+                    )
+            load_x_rows(2, even_images, nc.sync)
+            load_x_rows(2, odd_images, nc.scalar)
+
+        with tc.tile_pool(name="late", bufs=2) as late:
+            dws = late.tile([P, U_TILES, D], F32, bufs=1)
+            c_part = const.tile([P, U_TILES, SHIFTS], F32)
+
+            with tc.psum_pool(name="acc_psum", bufs=8) as acc_psum:
+                for s in range(SHIFTS):
+                    if s + LEAD < SHIFTS:
+                        prepare_xn(s + LEAD)
+                    for ub in range(U_TILES):
+                        acc = acc_psum.tile([P, C], F32)
+                        for g in range(PASSES):
+                            nc.tensor.matmul_mx(
+                                out=acc[:],
+                                lhsT=d_codes[:, g, u_cols(ub)].bitcast(E5M2_X4),
+                                lhsT_scale=d_scales[:, g, u_cols(ub)],
+                                rhs=xn_codes[s][:, g, :].bitcast(E4M3_X4),
+                                rhs_scale=xn_scales[s][:, g, :],
+                                start=(g == 0),
+                                stop=(g == PASSES - 1),
+                            )
+                        nc.scalar.activation(
+                            out=dws[:, ub, d_cols(s)], in_=acc[:], func=ACT.Copy, scale=a_col[:, ub : ub + 1]
+                        )
+                        products = late.tile([P, C], F32)
+                        nc.vector.scalar_tensor_tensor(
+                            out=products[:],
+                            in0=dws[:, ub, d_cols(s)],
+                            scalar=1.0,
+                            in1=w_t[:, ub, d_cols(s)],
+                            op0=ALU.mult,
+                            op1=ALU.mult,
+                            accum_out=c_part[:, ub, s : s + 1],
+                        )
+
+            neg_g = const.tile([P, U_TILES], F32)
+            nc.vector.reduce_sum(out=neg_g[:], in_=c_part[:], axis=mybir.AxisListType.X)
+            nc.vector.tensor_mul(out=neg_g[:], in0=neg_g[:], in1=neg_a_over_r[:])
+            with tc.psum_pool(name="out_psum", bufs=4) as out_psum:
+                for s in range(SHIFTS):
+                    for ub in range(U_TILES):
+                        nc.vector.scalar_tensor_tensor(
+                            out=dws[:, ub, d_cols(s)],
+                            in0=w_t[:, ub, d_cols(s)],
+                            scalar=neg_g[:, ub : ub + 1],
+                            in1=dws[:, ub, d_cols(s)],
+                            op0=ALU.mult,
+                            op1=ALU.add,
+                        )
+                    for pair in range(D_TILES_PER_SHIFT // 2):
+                        first_tile = s * D_TILES_PER_SHIFT + 2 * pair
+                        out_sb = xn_pool.tile([P, 2, U], F32, name="grouped", align_bytes=64)
+                        for t in range(2):
+                            d_tile = first_tile + t
+                            out_ps = out_psum.tile([P, U], F32)
+                            for ub in range(U_TILES):
+                                nc.tensor.transpose(
+                                    out_ps[:, u_cols(ub)], dws[:, ub, d_tile * P : (d_tile + 1) * P], ident_f32[:]
+                                )
+                            nc.scalar.copy(out=out_sb[:, t, :], in_=out_ps[:])
+                        nc.sync.dma_start(out=out_tiles[:, first_tile : first_tile + 2, :], in_=out_sb[:])

@@ -23,7 +23,7 @@ U_TILES = U // P
 D_TILES_PER_SHIFT = C // P
 P_SCALE, Q_SCALE, EPS, L2_EPS = 5.0, 0.3, 1e-6, 1e-12
 
-LEAD = 3
+LEAD = KS
 
 FLOPS = 2 * B * OY * OX * D * U
 
@@ -38,8 +38,8 @@ def tile_cossim2d_v_kernel(tc, x, w, p, q, x_rnorm, sim, grad_out, out):
     def u_cols(ub):
         return slice(ub * P, (ub + 1) * P)
 
-    def d_cols(s):
-        return slice(s * C, (s + 1) * C)
+    def d_cols(s, shifts=1):
+        return slice(s * C, (s + shifts) * C)
 
     def z_cols(g):
         return slice(g * PACK, (g + 1) * PACK)
@@ -54,20 +54,25 @@ def tile_cossim2d_v_kernel(tc, x, w, p, q, x_rnorm, sim, grad_out, out):
     ):
         x_rows = {}
 
-        def load_x_rows(i, images, queue):
-            if i not in x_rows:
-                x_rows[i] = x_pool.tile([P, W, C], BF16, name="x_rows")
+        def new_x_rows(i):
+            x_rows[i] = x_pool.tile([P, W, C], BF16, name="x_rows")
+
+        def load_x_rows(i, images, queue, columns=slice(0, W)):
             for b in images:
-                queue.dma_start(out=x_rows[i][b * OY : (b + 1) * OY, :, :], in_=x[b, i : i + OY, :, :])
+                queue.dma_start(
+                    out=x_rows[i][b * OY : (b + 1) * OY, columns, :], in_=x[b, i : i + OY, columns, :]
+                )
 
         even_images = range(0, B, 2)
         odd_images = range(1, B, 2)
 
+        def new_columns(g):
+            return slice(0 if g == 0 else g * PACK + KS - 1, (g + 1) * PACK + KS - 1)
+
         rnorm = const.tile([P, OX], F32)
         nc.sync.dma_start(out=rnorm[:], in_=x_rnorm.rearrange("b y z -> (b y) z"))
-        load_x_rows(0, even_images, nc.sync)
-        load_x_rows(0, odd_images, nc.scalar)
-
+        new_x_rows(0)
+        new_x_rows(1)
         p_rows = const.tile([P, P], BF16)
         nc.vector.memset(p_rows[:], 0.0)
         nc.scalar.dma_start(out=p_rows[0:U_TILES, :], in_=p.rearrange("(r c) -> r c", c=P))
@@ -78,6 +83,10 @@ def tile_cossim2d_v_kernel(tc, x, w, p, q, x_rnorm, sim, grad_out, out):
         make_identity(nc, ident_bf16[:])
         ident_f32 = const.tile([P, P], F32)
         make_identity(nc, ident_f32[:])
+        half = const.tile([P, U_TILES], F32)
+        nc.gpsimd.memset(half[:], 0.5)
+        minus_one = const.tile([P, U_TILES], F32)
+        nc.gpsimd.memset(minus_one[:], -1.0)
 
         w_t = keep.tile([P, U_TILES, D], BF16)
         d_codes = keep.tile([P, PASSES, U], U32, align_bytes=64)
@@ -86,30 +95,36 @@ def tile_cossim2d_v_kernel(tc, x, w, p, q, x_rnorm, sim, grad_out, out):
         xn_codes = {}
         xn_scales = {}
 
-        def prepare_xn(s):
-            i, j = divmod(s, KS)
+        def new_xn_codes(s):
             xn_codes[s] = code_pool.tile([P, PASSES, C], U32, name="xn_codes", align_bytes=64)
             xn_scales[s] = code_pool.tile([P, PASSES, C], U8, name="xn_scales", align_bytes=64)
+
+        def prepare_xn(units):
             grouped = {}
-            for g in range(PASSES):
+            for n, (s, g) in enumerate(units):
+                i, j = divmod(s, KS)
                 planes = xn_pool.tile([P, PACK, C], BF16, name="planes", bufs=3)
                 for t in range(PACK):
                     z = g * PACK + t
                     nc.vector.tensor_scalar_mul(
                         out=planes[:, t, :], in0=x_rows[i][:, z + j, :], scalar1=rnorm[:, z : z + 1]
                     )
-                grouped[g] = xn_pool.tile([P, C, PACK], BF16, name="grouped", align_bytes=64)
-                copier = nc.scalar.copy if (s > LEAD and g % 2 == 0) else nc.vector.tensor_copy
+                grouped[n] = xn_pool.tile([P, C, PACK], BF16, name="grouped", align_bytes=64)
+                copier = nc.scalar.copy if (s > LEAD and n % 2 == 0) else nc.vector.tensor_copy
                 copier(
-                    out=grouped[g][:].rearrange("p (c r) t -> p c t r", r=4),
+                    out=grouped[n][:].rearrange("p (c r) t -> p c t r", r=4),
                     in_=planes[:].rearrange("p t (c r) -> p c t r", r=4),
                 )
-            for g in range(PASSES):
+            for n, (s, g) in enumerate(units):
                 nc.vector.quantize_mx(
                     out=xn_codes[s][:, g, :].bitcast(E4M3_X4),
                     scales=xn_scales[s][:, g, :],
-                    in_=grouped[g][:].rearrange("p c t -> p (c t)"),
+                    in_=grouped[n][:].rearrange("p c t -> p (c t)"),
                 )
+
+        def prepare_xn_shift(s):
+            new_xn_codes(s)
+            prepare_xn([(s, g) for g in range(PASSES)])
 
         a_col = const.tile([P, U_TILES], F32)
         neg_a_over_r = const.tile([P, U_TILES], F32)
@@ -118,6 +133,12 @@ def tile_cossim2d_v_kernel(tc, x, w, p, q, x_rnorm, sim, grad_out, out):
             tc.tile_pool(name="early", bufs=2) as early,
             tc.psum_pool(name="early_psum", bufs=4) as early_psum,
         ):
+            sim_sb = {}
+            for g in range(PASSES):
+                load_x_rows(0, even_images, nc.sync, new_columns(g))
+                load_x_rows(0, odd_images, nc.scalar, new_columns(g))
+                sim_sb[g] = early.tile([P, PACK, U], F32, name="sim_sb", tag="stream", bufs=PASSES)
+                nc.sync.dma_start(out=sim_sb[g][:], in_=sim_rows[:, z_cols(g), :])
             go_sb = early.tile([P, OX, U], BF16, bufs=1)
             power = early.tile([P, U_TILES, OX, P], F32, bufs=1)
 
@@ -131,51 +152,19 @@ def tile_cossim2d_v_kernel(tc, x, w, p, q, x_rnorm, sim, grad_out, out):
             nc.scalar.activation(out=qq_col[:], in_=q_col[:], func=ACT.Square, scale=1.0 / Q_SCALE)
 
             for g in range(PASSES):
-                sim_sb = early.tile([P, PACK, U], F32)
-                nc.sync.dma_start(out=sim_sb[:], in_=sim_rows[:, z_cols(g), :])
                 for ub in range(U_TILES):
                     sim_t = early_psum.tile([P, PACK, P], F32, tag="turn")
                     for t in range(PACK):
-                        nc.tensor.transpose(sim_t[:, t, :], sim_sb[:, t, u_cols(ub)], ident_f32[:])
+                        nc.tensor.transpose(sim_t[:, t, :], sim_sb[g][:, t, u_cols(ub)], ident_f32[:])
                     nc.scalar.activation(out=power[:, ub, z_cols(g), :], in_=sim_t[:], func=ACT.Abs)
             nc.sync.dma_start(out=go_sb[:], in_=go_rows)
+            load_x_rows(1, even_images, nc.sync)
             load_x_rows(1, odd_images, nc.scalar)
 
-            r2_ps = [
-                early_psum.tile([P, P], F32, name="r2_ps%d" % ub, bufs=1) for ub in range(U_TILES)
-            ]
-            for s in range(SHIFTS):
-                w_sb = early.tile([P, D_TILES_PER_SHIFT, U], BF16, name="w_sb", bufs=3)
-                nc.sync.dma_start(
-                    out=w_sb[:], in_=w_tiles[:, s * D_TILES_PER_SHIFT : (s + 1) * D_TILES_PER_SHIFT, :]
-                )
-                for ub in range(U_TILES):
-                    for t in range(D_TILES_PER_SHIFT):
-                        nc.tensor.matmul(
-                            out=r2_ps[ub][:],
-                            lhsT=w_sb[:, t, u_cols(ub)],
-                            rhs=w_sb[:, t, u_cols(ub)],
-                            start=(s == 0 and t == 0),
-                            stop=(s == SHIFTS - 1 and t == D_TILES_PER_SHIFT - 1),
-                        )
-            load_x_rows(1, even_images, nc.sync)
-
             for s in range(LEAD):
-                prepare_xn(s)
-
-            r2_col = const.tile([P, U_TILES], F32)
-            for ub in range(U_TILES):
-                off_diagonal_zeroed = early.tile([P, P], F32)
-                nc.vector.scalar_tensor_tensor(
-                    out=off_diagonal_zeroed[:],
-                    in0=r2_ps[ub][:],
-                    scalar=1.0,
-                    in1=ident_f32[:],
-                    op0=ALU.mult,
-                    op1=ALU.mult,
-                    accum_out=r2_col[:, ub : ub + 1],
-                )
-            nc.vector.tensor_scalar_max(out=r2_col[:], in0=r2_col[:], scalar1=L2_EPS)
+                new_xn_codes(s)
+            for g in range(PASSES):
+                prepare_xn([(s, g) for s in range(LEAD)])
 
             ln_e = const.tile([P, U_TILES], F32)
             nc.scalar.activation(out=ln_e[:], in_=e_col[:], func=ACT.Ln)
@@ -207,17 +196,11 @@ def tile_cossim2d_v_kernel(tc, x, w, p, q, x_rnorm, sim, grad_out, out):
                     in_=d_grouped[:].rearrange("p u t -> p (u t)"),
                 )
 
-            r_col = const.tile([P, U_TILES], F32)
-            nc.scalar.activation(out=r_col[:], in_=r2_col[:], func=ACT.Sqrt)
-            w_norm = const.tile([P, U_TILES], F32)
-            nc.vector.tensor_scalar_add(out=w_norm[:], in0=r_col[:], scalar1=qq_col[:, 0:1])
-            nc.vector.reciprocal(out=a_col[:], in_=w_norm[:])
-            nc.vector.tensor_mul(out=w_norm[:], in0=w_norm[:], in1=r_col[:])
-            nc.vector.reciprocal(out=neg_a_over_r[:], in_=w_norm[:])
-            nc.vector.tensor_scalar_mul(out=neg_a_over_r[:], in0=neg_a_over_r[:], scalar1=-1.0)
-
+            r2_ps = [
+                early_psum.tile([P, P], F32, name="r2_ps%d" % ub, bufs=1) for ub in range(U_TILES)
+            ]
             for s in range(SHIFTS):
-                w_sb = early.tile([P, D_TILES_PER_SHIFT, U], BF16, name="w_sb", bufs=3)
+                w_sb = early.tile([P, D_TILES_PER_SHIFT, U], BF16, tag="stream", bufs=PASSES)
                 nc.sync.dma_start(
                     out=w_sb[:], in_=w_tiles[:, s * D_TILES_PER_SHIFT : (s + 1) * D_TILES_PER_SHIFT, :]
                 )
@@ -228,19 +211,52 @@ def tile_cossim2d_v_kernel(tc, x, w, p, q, x_rnorm, sim, grad_out, out):
                     nc.scalar.copy(
                         out=w_t[:, ub, d_cols(s)].rearrange("p (t d) -> p t d", d=P), in_=w_turn[:]
                     )
+                    for t in range(D_TILES_PER_SHIFT):
+                        nc.tensor.matmul(
+                            out=r2_ps[ub][:],
+                            lhsT=w_sb[:, t, u_cols(ub)],
+                            rhs=w_sb[:, t, u_cols(ub)],
+                            start=(s == 0 and t == 0),
+                            stop=(s == SHIFTS - 1 and t == D_TILES_PER_SHIFT - 1),
+                        )
+            new_x_rows(2)
             load_x_rows(2, even_images, nc.sync)
             load_x_rows(2, odd_images, nc.scalar)
 
-        with tc.tile_pool(name="late", bufs=2) as late:
-            dws = late.tile([P, U_TILES, D], F32, bufs=1)
-            c_part = const.tile([P, U_TILES, SHIFTS], F32)
+            prepare_xn_shift(LEAD)
 
-            with tc.psum_pool(name="acc_psum", bufs=8) as acc_psum:
-                for s in range(SHIFTS):
-                    if s + LEAD < SHIFTS:
-                        prepare_xn(s + LEAD)
+            r2_col = const.tile([P, U_TILES], F32)
+            for ub in range(U_TILES):
+                off_diagonal_zeroed = early.tile([P, P], F32)
+                nc.vector.scalar_tensor_tensor(
+                    out=off_diagonal_zeroed[:],
+                    in0=r2_ps[ub][:],
+                    scalar=1.0,
+                    in1=ident_f32[:],
+                    op0=ALU.mult,
+                    op1=ALU.mult,
+                    accum_out=r2_col[:, ub : ub + 1],
+                )
+            nc.gpsimd.tensor_scalar_max(out=r2_col[:], in0=r2_col[:], scalar1=L2_EPS)
+            r_col = const.tile([P, U_TILES], F32)
+            nc.gpsimd.tensor_tensor(out=r_col[:], in0=r2_col[:], in1=half[:], op=ALU.pow)
+            w_norm = const.tile([P, U_TILES], F32)
+            nc.gpsimd.tensor_scalar_add(out=w_norm[:], in0=r_col[:], scalar1=qq_col[:, 0:1])
+            nc.gpsimd.tensor_tensor(out=a_col[:], in0=w_norm[:], in1=minus_one[:], op=ALU.pow)
+            w_norm_r = const.tile([P, U_TILES], F32)
+            nc.gpsimd.tensor_tensor(out=w_norm_r[:], in0=w_norm[:], in1=r_col[:], op=ALU.mult)
+            nc.gpsimd.tensor_tensor(out=neg_a_over_r[:], in0=w_norm_r[:], in1=minus_one[:], op=ALU.pow)
+            nc.gpsimd.tensor_scalar_mul(out=neg_a_over_r[:], in0=neg_a_over_r[:], scalar1=-1.0)
+
+        with tc.tile_pool(name="late", bufs=1) as late:
+            dws = late.tile([P, U_TILES, D], F32)
+
+            with tc.psum_pool(name="acc_psum", bufs=8, reuse_waits="tile") as acc_psum:
+
+                def multiply(s):
+                    banks = []
                     for ub in range(U_TILES):
-                        acc = acc_psum.tile([P, C], F32)
+                        acc = acc_psum.tile([P, C], F32, name="acc")
                         for g in range(PASSES):
                             nc.tensor.matmul_mx(
                                 out=acc[:],
@@ -251,19 +267,34 @@ def tile_cossim2d_v_kernel(tc, x, w, p, q, x_rnorm, sim, grad_out, out):
                                 start=(g == 0),
                                 stop=(g == PASSES - 1),
                             )
+                        banks.append(acc)
+                    return banks
+
+                for s in range(SHIFTS):
+                    banks = multiply(s)
+                    if s + LEAD + 1 < SHIFTS:
+                        prepare_xn_shift(s + LEAD + 1)
+                    for ub in range(U_TILES):
                         nc.scalar.activation(
-                            out=dws[:, ub, d_cols(s)], in_=acc[:], func=ACT.Copy, scale=a_col[:, ub : ub + 1]
+                            out=dws[:, ub, d_cols(s)],
+                            in_=banks[ub][:],
+                            func=ACT.Copy,
+                            scale=a_col[:, ub : ub + 1],
                         )
-                        products = late.tile([P, C], F32)
-                        nc.vector.scalar_tensor_tensor(
-                            out=products[:],
-                            in0=dws[:, ub, d_cols(s)],
-                            scalar=1.0,
-                            in1=w_t[:, ub, d_cols(s)],
-                            op0=ALU.mult,
-                            op1=ALU.mult,
-                            accum_out=c_part[:, ub, s : s + 1],
-                        )
+
+            c_part = const.tile([P, U_TILES, KS], F32)
+            for i in range(KS):
+                for ub in range(U_TILES):
+                    products = code_pool.tile([P, KS * C], F32, name="xn_codes", align_bytes=64)
+                    nc.vector.scalar_tensor_tensor(
+                        out=products[:],
+                        in0=dws[:, ub, d_cols(i * KS, KS)],
+                        scalar=1.0,
+                        in1=w_t[:, ub, d_cols(i * KS, KS)],
+                        op0=ALU.mult,
+                        op1=ALU.mult,
+                        accum_out=c_part[:, ub, i : i + 1],
+                    )
 
             neg_g = const.tile([P, U_TILES], F32)
             nc.vector.reduce_sum(out=neg_g[:], in_=c_part[:], axis=mybir.AxisListType.X)

@@ -23,7 +23,7 @@ U_TILES = U // P
 D_TILES_PER_SHIFT = C // P
 P_SCALE, Q_SCALE, EPS, L2_EPS = 5.0, 0.3, 1e-6, 1e-12
 
-LEAD = KS
+LEAD = 4
 
 FLOPS = 2 * B * OY * OX * D * U
 
@@ -50,7 +50,7 @@ def tile_cossim2d_v_kernel(tc, x, w, p, q, x_rnorm, sim, grad_out, out):
         tc.tile_pool(name="keep", bufs=1) as keep,
         tc.tile_pool(name="x_pool", bufs=2) as x_pool,
         tc.tile_pool(name="xn_pool", bufs=4) as xn_pool,
-        tc.tile_pool(name="code_pool", bufs=LEAD + 1) as code_pool,
+        tc.tile_pool(name="code_pool", bufs=LEAD) as code_pool,
     ):
         x_rows = {}
 
@@ -99,22 +99,33 @@ def tile_cossim2d_v_kernel(tc, x, w, p, q, x_rnorm, sim, grad_out, out):
             xn_codes[s] = code_pool.tile([P, PASSES, C], U32, name="xn_codes", align_bytes=64)
             xn_scales[s] = code_pool.tile([P, PASSES, C], U8, name="xn_scales", align_bytes=64)
 
-        def prepare_xn(units):
-            grouped = {}
-            for n, (s, g) in enumerate(units):
-                i, j = divmod(s, KS)
-                planes = xn_pool.tile([P, PACK, C], BF16, name="planes", bufs=3)
-                for t in range(PACK):
-                    z = g * PACK + t
-                    nc.vector.tensor_scalar_mul(
-                        out=planes[:, t, :], in0=x_rows[i][:, z + j, :], scalar1=rnorm[:, z : z + 1]
-                    )
-                grouped[n] = xn_pool.tile([P, C, PACK], BF16, name="grouped", align_bytes=64)
-                copier = nc.scalar.copy if (s > LEAD and n % 2 == 0) else nc.vector.tensor_copy
-                copier(
-                    out=grouped[n][:].rearrange("p (c r) t -> p c t r", r=4),
-                    in_=planes[:].rearrange("p t (c r) -> p c t r", r=4),
+        def multiply_by_rnorm(s, g):
+            i, j = divmod(s, KS)
+            planes = xn_pool.tile([P, PACK, C], BF16, name="planes", bufs=3)
+            for t in range(PACK):
+                z = g * PACK + t
+                nc.vector.tensor_scalar_mul(
+                    out=planes[:, t, :], in0=x_rows[i][:, z + j, :], scalar1=rnorm[:, z : z + 1]
                 )
+            return planes
+
+        def regroup(planes, copier):
+            grouped = xn_pool.tile([P, C, PACK], BF16, name="grouped", align_bytes=64)
+            copier(
+                out=grouped[:].rearrange("p (c r) t -> p c t r", r=4),
+                in_=planes[:].rearrange("p t (c r) -> p c t r", r=4),
+            )
+            return grouped
+
+        def prepare_xn(units):
+            planes = {}
+            grouped = {}
+            for n in range(len(units) + 1):
+                if n < len(units):
+                    planes[n] = multiply_by_rnorm(*units[n])
+                if n > 0:
+                    shared = units[n - 1][0] >= LEAD and n % 2 == 1
+                    grouped[n - 1] = regroup(planes[n - 1], nc.scalar.copy if shared else nc.vector.tensor_copy)
             for n, (s, g) in enumerate(units):
                 nc.vector.quantize_mx(
                     out=xn_codes[s][:, g, :].bitcast(E4M3_X4),
@@ -134,11 +145,15 @@ def tile_cossim2d_v_kernel(tc, x, w, p, q, x_rnorm, sim, grad_out, out):
             tc.psum_pool(name="early_psum", bufs=4) as early_psum,
         ):
             sim_sb = {}
-            for g in range(PASSES):
+
+            def load_pass(g):
                 load_x_rows(0, even_images, nc.sync, new_columns(g))
                 load_x_rows(0, odd_images, nc.scalar, new_columns(g))
                 sim_sb[g] = early.tile([P, PACK, U], F32, name="sim_sb", tag="stream", bufs=PASSES)
                 nc.sync.dma_start(out=sim_sb[g][:], in_=sim_rows[:, z_cols(g), :])
+
+            load_pass(0)
+            load_pass(1)
             go_sb = early.tile([P, OX, U], BF16, bufs=1)
             power = early.tile([P, U_TILES, OX, P], F32, bufs=1)
 
@@ -157,22 +172,33 @@ def tile_cossim2d_v_kernel(tc, x, w, p, q, x_rnorm, sim, grad_out, out):
                     for t in range(PACK):
                         nc.tensor.transpose(sim_t[:, t, :], sim_sb[g][:, t, u_cols(ub)], ident_f32[:])
                     nc.scalar.activation(out=power[:, ub, z_cols(g), :], in_=sim_t[:], func=ACT.Abs)
+                if g + 2 < PASSES:
+                    load_pass(g + 2)
             nc.sync.dma_start(out=go_sb[:], in_=go_rows)
             load_x_rows(1, even_images, nc.sync)
             load_x_rows(1, odd_images, nc.scalar)
 
-            for s in range(LEAD):
+            for s in range(KS):
                 new_xn_codes(s)
             for g in range(PASSES):
-                prepare_xn([(s, g) for s in range(LEAD)])
+                prepare_xn([(s, g) for s in range(KS)])
 
             ln_e = const.tile([P, U_TILES], F32)
             nc.scalar.activation(out=ln_e[:], in_=e_col[:], func=ACT.Ln)
             for ub in range(U_TILES):
                 nc.scalar.activation(out=power[:, ub], in_=power[:, ub], func=ACT.Ln, bias=EPS)
 
+            d_grouped = {}
+
+            def quantise_dsim(g):
+                nc.vector.quantize_mx(
+                    out=d_codes[:, g, :].bitcast(E5M2_X4),
+                    scales=d_scales[:, g, :],
+                    in_=d_grouped[g][:].rearrange("p u t -> p (u t)"),
+                )
+
             for g in range(PASSES):
-                d_grouped = xn_pool.tile([P, U, PACK], BF16, name="grouped", align_bytes=64)
+                d_grouped[g] = xn_pool.tile([P, U, PACK], BF16, name="grouped", align_bytes=64)
                 for ub in range(U_TILES):
                     nc.scalar.activation(
                         out=power[:, ub, z_cols(g), :],
@@ -185,16 +211,14 @@ def tile_cossim2d_v_kernel(tc, x, w, p, q, x_rnorm, sim, grad_out, out):
                     for t in range(PACK):
                         nc.tensor.transpose(power_rows[:, t, :], power[:, ub, g * PACK + t, :], ident_f32[:])
                     nc.vector.tensor_tensor(
-                        out=d_grouped[:, u_cols(ub), :],
+                        out=d_grouped[g][:, u_cols(ub), :],
                         in0=power_rows[:].rearrange("p t u -> p u t"),
                         in1=go_sb[:, z_cols(g), u_cols(ub)].rearrange("p t u -> p u t"),
                         op=ALU.mult,
                     )
-                nc.vector.quantize_mx(
-                    out=d_codes[:, g, :].bitcast(E5M2_X4),
-                    scales=d_scales[:, g, :],
-                    in_=d_grouped[:].rearrange("p u t -> p (u t)"),
-                )
+                if g > 0:
+                    quantise_dsim(g - 1)
+            quantise_dsim(PASSES - 1)
 
             r2_ps = [
                 early_psum.tile([P, P], F32, name="r2_ps%d" % ub, bufs=1) for ub in range(U_TILES)
@@ -223,7 +247,8 @@ def tile_cossim2d_v_kernel(tc, x, w, p, q, x_rnorm, sim, grad_out, out):
             load_x_rows(2, even_images, nc.sync)
             load_x_rows(2, odd_images, nc.scalar)
 
-            prepare_xn_shift(LEAD)
+            for s in range(KS, LEAD):
+                prepare_xn_shift(s)
 
             r2_col = const.tile([P, U_TILES], F32)
             for ub in range(U_TILES):
@@ -272,8 +297,8 @@ def tile_cossim2d_v_kernel(tc, x, w, p, q, x_rnorm, sim, grad_out, out):
 
                 for s in range(SHIFTS):
                     banks = multiply(s)
-                    if s + LEAD + 1 < SHIFTS:
-                        prepare_xn_shift(s + LEAD + 1)
+                    if s + LEAD < SHIFTS:
+                        prepare_xn_shift(s + LEAD)
                     for ub in range(U_TILES):
                         nc.scalar.activation(
                             out=dws[:, ub, d_cols(s)],

@@ -23,7 +23,7 @@ U_TILES = U // P
 D_TILES_PER_SHIFT = C // P
 P_SCALE, Q_SCALE, EPS, L2_EPS = 5.0, 0.3, 1e-6, 1e-12
 
-LEAD = 4
+LEAD = 5
 
 FLOPS = 2 * B * OY * OX * D * U
 
@@ -149,7 +149,7 @@ def tile_cossim2d_v_kernel(tc, x, w, p, q, x_rnorm, sim, grad_out, out):
             def load_pass(g):
                 load_x_rows(0, even_images, nc.sync, new_columns(g))
                 load_x_rows(0, odd_images, nc.scalar, new_columns(g))
-                sim_sb[g] = early.tile([P, PACK, U], F32, name="sim_sb", tag="stream", bufs=PASSES)
+                sim_sb[g] = early.tile([P, PACK, U], F32, name="sim_sb", tag="stream", bufs=3)
                 nc.sync.dma_start(out=sim_sb[g][:], in_=sim_rows[:, z_cols(g), :])
 
             load_pass(0)
@@ -224,7 +224,7 @@ def tile_cossim2d_v_kernel(tc, x, w, p, q, x_rnorm, sim, grad_out, out):
                 early_psum.tile([P, P], F32, name="r2_ps%d" % ub, bufs=1) for ub in range(U_TILES)
             ]
             for s in range(SHIFTS):
-                w_sb = early.tile([P, D_TILES_PER_SHIFT, U], BF16, tag="stream", bufs=PASSES)
+                w_sb = early.tile([P, D_TILES_PER_SHIFT, U], BF16, tag="stream", bufs=3)
                 nc.sync.dma_start(
                     out=w_sb[:], in_=w_tiles[:, s * D_TILES_PER_SHIFT : (s + 1) * D_TILES_PER_SHIFT, :]
                 )
@@ -247,15 +247,21 @@ def tile_cossim2d_v_kernel(tc, x, w, p, q, x_rnorm, sim, grad_out, out):
             load_x_rows(2, even_images, nc.sync)
             load_x_rows(2, odd_images, nc.scalar)
 
+            r2_blocks = const.tile([P, U_TILES, P], F32)
+            for ub in range(U_TILES):
+                nc.scalar.copy(out=r2_blocks[:, ub, :], in_=r2_ps[ub][:])
+
+        with tc.tile_pool(name="late", bufs=1) as late:
+            dws = late.tile([P, U_TILES, D], F32)
+
             for s in range(KS, LEAD):
                 prepare_xn_shift(s)
 
             r2_col = const.tile([P, U_TILES], F32)
             for ub in range(U_TILES):
-                off_diagonal_zeroed = early.tile([P, P], F32)
                 nc.vector.scalar_tensor_tensor(
-                    out=off_diagonal_zeroed[:],
-                    in0=r2_ps[ub][:],
+                    out=r2_blocks[:, ub, :],
+                    in0=r2_blocks[:, ub, :],
                     scalar=1.0,
                     in1=ident_f32[:],
                     op0=ALU.mult,
@@ -272,9 +278,6 @@ def tile_cossim2d_v_kernel(tc, x, w, p, q, x_rnorm, sim, grad_out, out):
             nc.gpsimd.tensor_tensor(out=w_norm_r[:], in0=w_norm[:], in1=r_col[:], op=ALU.mult)
             nc.gpsimd.tensor_tensor(out=neg_a_over_r[:], in0=w_norm_r[:], in1=minus_one[:], op=ALU.pow)
             nc.gpsimd.tensor_scalar_mul(out=neg_a_over_r[:], in0=neg_a_over_r[:], scalar1=-1.0)
-
-        with tc.tile_pool(name="late", bufs=1) as late:
-            dws = late.tile([P, U_TILES, D], F32)
 
             with tc.psum_pool(name="acc_psum", bufs=8, reuse_waits="tile") as acc_psum:
 

@@ -63,6 +63,11 @@ def tile_cossim2d_v_kernel(tc, x, w, p, q, x_rnorm, sim, grad_out, out):
                     out=x_rows[i][b * OY : (b + 1) * OY, columns, :], in_=x[b, i : i + OY, columns, :]
                 )
 
+        def shift_x_rows(i):
+            for first, end in ((0, 64), (64, 112), (112, 127)):
+                nc.sync.dma_start(out=x_rows[i][first:end], in_=x_rows[i - 1][first + 1 : end + 1])
+            nc.sync.dma_start(out=x_rows[i][OY - 1 : P : OY], in_=x[:, i + OY - 1])
+
         even_images = range(0, B, 2)
         odd_images = range(1, B, 2)
 
@@ -175,8 +180,7 @@ def tile_cossim2d_v_kernel(tc, x, w, p, q, x_rnorm, sim, grad_out, out):
                 if g + 2 < PASSES:
                     load_pass(g + 2)
             nc.sync.dma_start(out=go_sb[:], in_=go_rows)
-            load_x_rows(1, even_images, nc.sync)
-            load_x_rows(1, odd_images, nc.scalar)
+            shift_x_rows(1)
 
             for s in range(KS):
                 new_xn_codes(s)
@@ -244,8 +248,7 @@ def tile_cossim2d_v_kernel(tc, x, w, p, q, x_rnorm, sim, grad_out, out):
                             stop=(s == SHIFTS - 1 and t == D_TILES_PER_SHIFT - 1),
                         )
             new_x_rows(2)
-            load_x_rows(2, even_images, nc.sync)
-            load_x_rows(2, odd_images, nc.scalar)
+            shift_x_rows(2)
 
             r2_blocks = const.tile([P, U_TILES, P], F32)
             for ub in range(U_TILES):

@@ -171,12 +171,18 @@ def tile_cossim2d_v_kernel(tc, x, w, p, q, x_rnorm, sim, grad_out, out):
             qq_col = const.tile([P, 1], F32)
             nc.scalar.activation(out=qq_col[:], in_=q_col[:], func=ACT.Square, scale=1.0 / Q_SCALE)
 
+            ln_e = const.tile([P, U_TILES], F32)
+            nc.scalar.activation(out=ln_e[:], in_=e_col[:], func=ACT.Ln)
+
             for g in range(PASSES):
                 for ub in range(U_TILES):
                     sim_t = early_psum.tile([P, PACK, P], F32, tag="turn")
                     for t in range(PACK):
                         nc.tensor.transpose(sim_t[:, t, :], sim_sb[g][:, t, u_cols(ub)], ident_f32[:])
                     nc.scalar.activation(out=power[:, ub, z_cols(g), :], in_=sim_t[:], func=ACT.Abs)
+                nc.scalar.activation(
+                    out=power[:, :, z_cols(g), :], in_=power[:, :, z_cols(g), :], func=ACT.Ln, bias=EPS
+                )
                 if g + 2 < PASSES:
                     load_pass(g + 2)
             nc.sync.dma_start(out=go_sb[:], in_=go_rows)
@@ -186,11 +192,6 @@ def tile_cossim2d_v_kernel(tc, x, w, p, q, x_rnorm, sim, grad_out, out):
                 new_xn_codes(s)
             for g in range(PASSES):
                 prepare_xn([(s, g) for s in range(KS)])
-
-            ln_e = const.tile([P, U_TILES], F32)
-            nc.scalar.activation(out=ln_e[:], in_=e_col[:], func=ACT.Ln)
-            for ub in range(U_TILES):
-                nc.scalar.activation(out=power[:, ub], in_=power[:, ub], func=ACT.Ln, bias=EPS)
 
             d_grouped = {}
 

@@ -117,8 +117,8 @@ def tile_cossim2d_v_kernel(tc, x, w, p, q, x_rnorm, sim, grad_out, out):
         def regroup(planes, copier):
             grouped = xn_pool.tile([P, C, PACK], BF16, name="grouped", align_bytes=64)
             copier(
-                out=grouped[:].rearrange("p (c r) t -> p c t r", r=4),
-                in_=planes[:].rearrange("p t (c r) -> p c t r", r=4),
+                out=grouped[:].rearrange("p (c r) t -> p c t r", r=2),
+                in_=planes[:].rearrange("p t (c r) -> p c t r", r=2),
             )
             return grouped
 
@@ -180,11 +180,11 @@ def tile_cossim2d_v_kernel(tc, x, w, p, q, x_rnorm, sim, grad_out, out):
                     for t in range(PACK):
                         nc.tensor.transpose(sim_t[:, t, :], sim_sb[g][:, t, u_cols(ub)], ident_f32[:])
                     nc.scalar.activation(out=power[:, ub, z_cols(g), :], in_=sim_t[:], func=ACT.Abs)
+                if g + 2 < PASSES:
+                    load_pass(g + 2)
                 nc.scalar.activation(
                     out=power[:, :, z_cols(g), :], in_=power[:, :, z_cols(g), :], func=ACT.Ln, bias=EPS
                 )
-                if g + 2 < PASSES:
-                    load_pass(g + 2)
             nc.sync.dma_start(out=go_sb[:], in_=go_rows)
             shift_x_rows(1)
 

@@ -93,7 +93,9 @@ def tile_cossim2d_v_kernel(tc, x, w, p, q, x_rnorm, sim, grad_out, out):
         minus_one = const.tile([P, U_TILES], F32)
         nc.gpsimd.memset(minus_one[:], -1.0)
 
-        w_t = keep.tile([P, U_TILES, D], BF16)
+        w_t_first = keep.tile([P, KS, U_TILES, C], BF16)
+        w_t_rest = []
+        first_planes = keep.tile([P, 2, PACK, KS, C], BF16, name="first_planes", tag="w_t_rest")
         d_codes = keep.tile([P, PASSES, U], U32, align_bytes=64)
         d_scales = keep.tile([P, PASSES, U], U8, align_bytes=64)
 
@@ -104,43 +106,63 @@ def tile_cossim2d_v_kernel(tc, x, w, p, q, x_rnorm, sim, grad_out, out):
             xn_codes[s] = code_pool.tile([P, PASSES, C], U32, name="xn_codes", align_bytes=64)
             xn_scales[s] = code_pool.tile([P, PASSES, C], U8, name="xn_scales", align_bytes=64)
 
-        def multiply_by_rnorm(s, g):
-            i, j = divmod(s, KS)
-            planes = xn_pool.tile([P, PACK, C], BF16, name="planes", bufs=3)
+        def multiply_by_rnorm(planes, shifts, g):
+            i, j = divmod(shifts[0], KS)
             for t in range(PACK):
                 z = g * PACK + t
                 nc.vector.tensor_scalar_mul(
-                    out=planes[:, t, :], in0=x_rows[i][:, z + j, :], scalar1=rnorm[:, z : z + 1]
+                    out=planes[:, t], in0=x_rows[i][:, z + j : z + j + len(shifts), :], scalar1=rnorm[:, z : z + 1]
                 )
-            return planes
 
         def regroup(planes, copier):
             grouped = xn_pool.tile([P, C, PACK], BF16, name="grouped", align_bytes=64)
             copier(
                 out=grouped[:].rearrange("p (c r) t -> p c t r", r=2),
-                in_=planes[:].rearrange("p t (c r) -> p c t r", r=2),
+                in_=planes.rearrange("p t (c r) -> p c t r", r=2),
             )
             return grouped
 
-        def prepare_xn(units):
-            planes = {}
-            grouped = {}
-            for n in range(len(units) + 1):
-                if n < len(units):
-                    planes[n] = multiply_by_rnorm(*units[n])
-                if n > 0:
-                    shared = units[n - 1][0] >= LEAD and n % 2 == 1
-                    grouped[n - 1] = regroup(planes[n - 1], nc.scalar.copy if shared else nc.vector.tensor_copy)
-            for n, (s, g) in enumerate(units):
-                nc.vector.quantize_mx(
-                    out=xn_codes[s][:, g, :].bitcast(E4M3_X4),
-                    scales=xn_scales[s][:, g, :],
-                    in_=grouped[n][:].rearrange("p c t -> p (c t)"),
-                )
+        def quantise(s, g, grouped):
+            nc.vector.quantize_mx(
+                out=xn_codes[s][:, g, :].bitcast(E4M3_X4),
+                scales=xn_scales[s][:, g, :],
+                in_=grouped[:].rearrange("p c t -> p (c t)"),
+            )
 
-        def prepare_xn_shift(s):
+        def prepare_pair(s, shared, between=None):
             new_xn_codes(s)
-            prepare_xn([(s, g) for g in range(PASSES)])
+            new_xn_codes(s + 1)
+            planes = {}
+            late = []
+            for g in range(PASSES + 1):
+                if g < PASSES:
+                    planes[g] = xn_pool.tile([P, PACK, 2, C], BF16, name="planes", bufs=2)
+                    multiply_by_rnorm(planes[g], (s, s + 1), g)
+                if g > 0:
+                    for shift, tile in late:
+                        quantise(*shift, tile)
+                    second = regroup(planes[g - 1][:, :, 1, :], nc.scalar.copy if shared else nc.vector.tensor_copy)
+                    first = regroup(planes[g - 1][:, :, 0, :], nc.vector.tensor_copy)
+                    late = [((s + 1, g - 1), second), ((s, g - 1), first)]
+                if between is not None and g == 2:
+                    between()
+            for shift, tile in late:
+                quantise(*shift, tile)
+
+        def prepare_single(s):
+            new_xn_codes(s)
+            regrouped = {}
+            planes = {}
+            for g in range(0, PASSES, 2):
+                planes[g] = xn_pool.tile([P, 2, PACK, 1, C], BF16, name="planes", bufs=2)
+                for h in range(2):
+                    multiply_by_rnorm(planes[g][:, h], (s,), g + h)
+            for g in range(PASSES):
+                regrouped[g] = regroup(
+                    planes[g - g % 2][:, g % 2, :, 0, :], nc.vector.tensor_copy if g % 2 else nc.scalar.copy
+                )
+            for g in (1, 0, 3, 2):
+                quantise(s, g, regrouped[g])
 
         a_col = const.tile([P, U_TILES], F32)
         neg_a_over_r = const.tile([P, U_TILES], F32)
@@ -174,6 +196,36 @@ def tile_cossim2d_v_kernel(tc, x, w, p, q, x_rnorm, sim, grad_out, out):
             ln_e = const.tile([P, U_TILES], F32)
             nc.scalar.activation(out=ln_e[:], in_=e_col[:], func=ACT.Ln)
 
+            r2_ps = [
+                early_psum.tile([P, P], F32, name="r2_ps%d" % ub, bufs=1) for ub in range(U_TILES)
+            ]
+            w_sb = {}
+
+            def load_w(s):
+                w_sb[s] = early.tile(
+                    [P, D_TILES_PER_SHIFT, U], BF16, name="w_sb", tag="stream", bufs=3
+                )
+                nc.sync.dma_start(
+                    out=w_sb[s][:], in_=w_tiles[:, s * D_TILES_PER_SHIFT : (s + 1) * D_TILES_PER_SHIFT, :]
+                )
+
+            def turn_w(s):
+                for ub in range(U_TILES):
+                    w_turn = early_psum.tile([P, D_TILES_PER_SHIFT, P], BF16, tag="turn")
+                    for t in range(D_TILES_PER_SHIFT):
+                        nc.tensor.transpose(w_turn[:, t, :], w_sb[s][:, t, u_cols(ub)], ident_bf16[:])
+                    nc.scalar.copy(
+                        out=w_t(s)[:, ub].rearrange("p (t d) -> p t d", d=P), in_=w_turn[:]
+                    )
+                    for t in range(D_TILES_PER_SHIFT):
+                        nc.tensor.matmul(
+                            out=r2_ps[ub][:],
+                            lhsT=w_sb[s][:, t, u_cols(ub)],
+                            rhs=w_sb[s][:, t, u_cols(ub)],
+                            start=(s == 0 and t == 0),
+                            stop=(s == SHIFTS - 1 and t == D_TILES_PER_SHIFT - 1),
+                        )
+
             for g in range(PASSES):
                 for ub in range(U_TILES):
                     sim_t = early_psum.tile([P, PACK, P], F32, tag="turn")
@@ -185,13 +237,32 @@ def tile_cossim2d_v_kernel(tc, x, w, p, q, x_rnorm, sim, grad_out, out):
                 nc.scalar.activation(
                     out=power[:, :, z_cols(g), :], in_=power[:, :, z_cols(g), :], func=ACT.Ln, bias=EPS
                 )
+            load_w(0)
             nc.sync.dma_start(out=go_sb[:], in_=go_rows)
             shift_x_rows(1)
 
+            first_grouped = {}
+
+            def w_t(s):
+                if s < KS:
+                    return w_t_first[:, s]
+                if not w_t_rest:
+                    w_t_rest.append(keep.tile([P, SHIFTS - KS, U_TILES, C], BF16, name="w_t_rest", tag="w_t_rest"))
+                return w_t_rest[0][:, s - KS]
+
+            def multiply_first(g):
+                multiply_by_rnorm(first_planes[:, g % 2], range(KS), g)
+
             for s in range(KS):
                 new_xn_codes(s)
+            multiply_first(0)
             for g in range(PASSES):
-                prepare_xn([(s, g) for s in range(KS)])
+                for s in range(KS):
+                    first_grouped[s, g] = regroup(first_planes[:, g % 2, :, s, :], nc.vector.tensor_copy)
+                if g + 1 < PASSES:
+                    multiply_first(g + 1)
+                for s in range(KS):
+                    quantise(s, g, first_grouped[s, g])
 
             d_grouped = {}
 
@@ -202,8 +273,8 @@ def tile_cossim2d_v_kernel(tc, x, w, p, q, x_rnorm, sim, grad_out, out):
                     in_=d_grouped[g][:].rearrange("p u t -> p (u t)"),
                 )
 
+            turn_w(0)
             for g in range(PASSES):
-                d_grouped[g] = xn_pool.tile([P, U, PACK], BF16, name="grouped", align_bytes=64)
                 for ub in range(U_TILES):
                     nc.scalar.activation(
                         out=power[:, ub, z_cols(g), :],
@@ -212,6 +283,9 @@ def tile_cossim2d_v_kernel(tc, x, w, p, q, x_rnorm, sim, grad_out, out):
                         scale=e_minus_1[:, ub : ub + 1],
                         bias=ln_e[:, ub : ub + 1],
                     )
+            for g in range(PASSES):
+                d_grouped[g] = xn_pool.tile([P, U, PACK], BF16, name="grouped", align_bytes=64)
+                for ub in range(U_TILES):
                     power_rows = early_psum.tile([P, PACK, P], F32, tag="turn")
                     for t in range(PACK):
                         nc.tensor.transpose(power_rows[:, t, :], power[:, ub, g * PACK + t, :], ident_f32[:])
@@ -225,29 +299,9 @@ def tile_cossim2d_v_kernel(tc, x, w, p, q, x_rnorm, sim, grad_out, out):
                     quantise_dsim(g - 1)
             quantise_dsim(PASSES - 1)
 
-            r2_ps = [
-                early_psum.tile([P, P], F32, name="r2_ps%d" % ub, bufs=1) for ub in range(U_TILES)
-            ]
-            for s in range(SHIFTS):
-                w_sb = early.tile([P, D_TILES_PER_SHIFT, U], BF16, tag="stream", bufs=3)
-                nc.sync.dma_start(
-                    out=w_sb[:], in_=w_tiles[:, s * D_TILES_PER_SHIFT : (s + 1) * D_TILES_PER_SHIFT, :]
-                )
-                for ub in range(U_TILES):
-                    w_turn = early_psum.tile([P, D_TILES_PER_SHIFT, P], BF16, tag="turn")
-                    for t in range(D_TILES_PER_SHIFT):
-                        nc.tensor.transpose(w_turn[:, t, :], w_sb[:, t, u_cols(ub)], ident_bf16[:])
-                    nc.scalar.copy(
-                        out=w_t[:, ub, d_cols(s)].rearrange("p (t d) -> p t d", d=P), in_=w_turn[:]
-                    )
-                    for t in range(D_TILES_PER_SHIFT):
-                        nc.tensor.matmul(
-                            out=r2_ps[ub][:],
-                            lhsT=w_sb[:, t, u_cols(ub)],
-                            rhs=w_sb[:, t, u_cols(ub)],
-                            start=(s == 0 and t == 0),
-                            stop=(s == SHIFTS - 1 and t == D_TILES_PER_SHIFT - 1),
-                        )
+            for s in range(1, SHIFTS):
+                load_w(s)
+                turn_w(s)
             new_x_rows(2)
             shift_x_rows(2)
 
@@ -258,8 +312,7 @@ def tile_cossim2d_v_kernel(tc, x, w, p, q, x_rnorm, sim, grad_out, out):
         with tc.tile_pool(name="late", bufs=1) as late:
             dws = late.tile([P, U_TILES, D], F32)
 
-            for s in range(KS, LEAD):
-                prepare_xn_shift(s)
+            prepare_pair(KS, shared=False)
 
             r2_col = const.tile([P, U_TILES], F32)
             for ub in range(U_TILES):
@@ -302,27 +355,47 @@ def tile_cossim2d_v_kernel(tc, x, w, p, q, x_rnorm, sim, grad_out, out):
                         banks.append(acc)
                     return banks
 
-                for s in range(SHIFTS):
-                    banks = multiply(s)
-                    if s + LEAD < SHIFTS:
-                        prepare_xn_shift(s + LEAD)
+                banks = {}
+
+                def multiply_shift(s):
+                    banks[s] = multiply(s)
+
+                def empty(s):
                     for ub in range(U_TILES):
                         nc.scalar.activation(
                             out=dws[:, ub, d_cols(s)],
-                            in_=banks[ub][:],
+                            in_=banks[s][ub][:],
                             func=ACT.Copy,
                             scale=a_col[:, ub : ub + 1],
                         )
+
+                def empty_and_go_on():
+                    empty(1)
+                    multiply_shift(3)
+
+                multiply_shift(0)
+                prepare_single(5)
+                empty(0)
+                multiply_shift(1)
+                multiply_shift(2)
+                prepare_pair(6, shared=True, between=empty_and_go_on)
+                empty(2)
+                multiply_shift(4)
+                prepare_single(8)
+                for s in range(3, SHIFTS):
+                    empty(s)
+                    if s + 2 < SHIFTS:
+                        multiply_shift(s + 2)
 
             c_part = const.tile([P, U_TILES, KS], F32)
             for i in range(KS):
                 for ub in range(U_TILES):
                     products = code_pool.tile([P, KS * C], F32, name="xn_codes", align_bytes=64)
                     nc.vector.scalar_tensor_tensor(
-                        out=products[:],
-                        in0=dws[:, ub, d_cols(i * KS, KS)],
+                        out=products[:].rearrange("p (s d) -> p s d", d=C),
+                        in0=dws[:, ub, d_cols(i * KS, KS)].rearrange("p (s d) -> p s d", d=C),
                         scalar=1.0,
-                        in1=w_t[:, ub, d_cols(i * KS, KS)],
+                        in1=(w_t_rest[0][:, (i - 1) * KS : i * KS] if i else w_t_first[:])[:, :, ub],
                         op0=ALU.mult,
                         op1=ALU.mult,
                         accum_out=c_part[:, ub, i : i + 1],
@@ -336,7 +409,7 @@ def tile_cossim2d_v_kernel(tc, x, w, p, q, x_rnorm, sim, grad_out, out):
                     for ub in range(U_TILES):
                         nc.vector.scalar_tensor_tensor(
                             out=dws[:, ub, d_cols(s)],
-                            in0=w_t[:, ub, d_cols(s)],
+                            in0=w_t(s)[:, ub],
                             scalar=neg_g[:, ub : ub + 1],
                             in1=dws[:, ub, d_cols(s)],
                             op0=ALU.mult,

import concourse.mybir as mybir
from concourse.masks import make_identity

F32 = mybir.dt.float32
BF16 = mybir.dt.bfloat16
U32 = mybir.dt.uint32
U8 = mybir.dt.uint8
E4M3_X4 = mybir.dt.float8_e4m3fn_x4
E5M2_X4 = mybir.dt.float8_e5m2_x4
ACT = mybir.ActivationFunctionType
ALU = mybir.AluOpType

P = 128
PACK = 4
B, H, W, C = 8, 18, 18, 512
KS = 3
OY, OX = H - KS + 1, W - KS + 1
U = 512
D = KS * KS * C
SHIFTS = KS * KS
PASSES = OX // PACK
U_TILES = U // P
D_TILES_PER_SHIFT = C // P
P_SCALE, Q_SCALE, EPS, L2_EPS = 5.0, 0.3, 1e-6, 1e-12

LEAD = 5

FLOPS = 2 * B * OY * OX * D * U


def tile_cossim2d_v_kernel(tc, x, w, p, q, x_rnorm, sim, grad_out, out):
    nc = tc.nc
    sim_rows = sim.rearrange("b y z u -> (b y) z u")
    go_rows = grad_out.rearrange("b y z u -> (b y) z u")
    w_tiles = w.rearrange("o (t p) u -> p (o t) u", p=P)
    out_tiles = out.rearrange("o (t p) u -> p (o t) u", p=P)

    def u_cols(ub):
        return slice(ub * P, (ub + 1) * P)

    def d_cols(s, shifts=1):
        return slice(s * C, (s + shifts) * C)

    def z_cols(g):
        return slice(g * PACK, (g + 1) * PACK)

    with (
        tc.manual_schedule(),
        tc.tile_pool(name="const", bufs=1) as const,
        tc.tile_pool(name="keep", bufs=1) as keep,
        tc.tile_pool(name="x_pool", bufs=2) as x_pool,
        tc.tile_pool(name="xn_pool", bufs=4) as xn_pool,
        tc.tile_pool(name="code_pool", bufs=LEAD) as code_pool,
    ):
        x_rows = {}

        def new_x_rows(i):
            x_rows[i] = x_pool.tile([P, W, C], BF16, name="x_rows")

        def load_x_rows(i, images, queue, columns=slice(0, W)):
            for b in images:
                queue.dma_start(
                    out=x_rows[i][b * OY : (b + 1) * OY, columns, :], in_=x[b, i : i + OY, columns, :]
                )

        def shift_x_rows(i):
            for first, end in ((0, 64), (64, 112), (112, 127)):
                nc.sync.dma_start(out=x_rows[i][first:end], in_=x_rows[i - 1][first + 1 : end + 1])
            nc.sync.dma_start(out=x_rows[i][OY - 1 : P : OY], in_=x[:, i + OY - 1])

        even_images = range(0, B, 2)
        odd_images = range(1, B, 2)

        def new_columns(g):
            return slice(0 if g == 0 else g * PACK + KS - 1, (g + 1) * PACK + KS - 1)

        rnorm = const.tile([P, OX], F32)
        nc.sync.dma_start(out=rnorm[:], in_=x_rnorm.rearrange("b y z -> (b y) z"))
        new_x_rows(0)
        new_x_rows(1)
        p_rows = const.tile([P, P], BF16)
        nc.vector.memset(p_rows[:], 0.0)
        nc.scalar.dma_start(out=p_rows[0:U_TILES, :], in_=p.rearrange("(r c) -> r c", c=P))
        q_col = const.tile([P, 1], BF16)
        nc.scalar.dma_start(out=q_col[:], in_=q.partition_broadcast(P))

        ident_bf16 = const.tile([P, P], BF16)
        make_identity(nc, ident_bf16[:])
        ident_f32 = const.tile([P, P], F32)
        make_identity(nc, ident_f32[:])
        half = const.tile([P, U_TILES], F32)
        nc.gpsimd.memset(half[:], 0.5)
        minus_one = const.tile([P, U_TILES], F32)
        nc.gpsimd.memset(minus_one[:], -1.0)

        w_t_first = keep.tile([P, KS, U_TILES, C], BF16)
        w_t_rest = []
        first_planes = keep.tile([P, 2, PACK, KS, C], BF16, name="first_planes", tag="w_t_rest")
        d_codes = keep.tile([P, PASSES, U], U32, align_bytes=64)
        d_scales = keep.tile([P, PASSES, U], U8, align_bytes=64)

        xn_codes = {}
        xn_scales = {}

        def new_xn_codes(s):
            xn_codes[s] = code_pool.tile([P, PASSES, C], U32, name="xn_codes", align_bytes=64)
            xn_scales[s] = code_pool.tile([P, PASSES, C], U8, name="xn_scales", align_bytes=64)

        def multiply_by_rnorm(planes, shifts, g):
            i, j = divmod(shifts[0], KS)
            for t in range(PACK):
                z = g * PACK + t
                nc.vector.tensor_scalar_mul(
                    out=planes[:, t], in0=x_rows[i][:, z + j : z + j + len(shifts), :], scalar1=rnorm[:, z : z + 1]
                )

        def regroup(planes, copier):
            grouped = xn_pool.tile([P, C, PACK], BF16, name="grouped", align_bytes=64)
            copier(
                out=grouped[:].rearrange("p (c r) t -> p c t r", r=2),
                in_=planes.rearrange("p t (c r) -> p c t r", r=2),
            )
            return grouped

        def quantise(s, g, grouped):
            nc.vector.quantize_mx(
                out=xn_codes[s][:, g, :].bitcast(E4M3_X4),
                scales=xn_scales[s][:, g, :],
                in_=grouped[:].rearrange("p c t -> p (c t)"),
            )

        def prepare_pair(s, shared, between=None):
            new_xn_codes(s)
            new_xn_codes(s + 1)
            planes = {}
            late = []
            for g in range(PASSES + 1):
                if g < PASSES:
                    planes[g] = xn_pool.tile([P, PACK, 2, C], BF16, name="planes", bufs=2)
                    multiply_by_rnorm(planes[g], (s, s + 1), g)
                if g > 0:
                    for shift, tile in late:
                        quantise(*shift, tile)
                    second = regroup(planes[g - 1][:, :, 1, :], nc.scalar.copy if shared else nc.vector.tensor_copy)
                    first = regroup(planes[g - 1][:, :, 0, :], nc.vector.tensor_copy)
                    late = [((s + 1, g - 1), second), ((s, g - 1), first)]
                if between is not None and g == 2:
                    between()
            for shift, tile in late:
                quantise(*shift, tile)

        def prepare_single(s):
            new_xn_codes(s)
            regrouped = {}
            planes = {}
            for g in range(0, PASSES, 2):
                planes[g] = xn_pool.tile([P, 2, PACK, 1, C], BF16, name="planes", bufs=2)
                for h in range(2):
                    multiply_by_rnorm(planes[g][:, h], (s,), g + h)
            for g in range(PASSES):
                regrouped[g] = regroup(
                    planes[g - g % 2][:, g % 2, :, 0, :], nc.vector.tensor_copy if g % 2 else nc.scalar.copy
                )
            for g in (1, 0, 3, 2):
                quantise(s, g, regrouped[g])

        a_col = const.tile([P, U_TILES], F32)
        neg_a_over_r = const.tile([P, U_TILES], F32)

        with (
            tc.tile_pool(name="early", bufs=2) as early,
            tc.psum_pool(name="early_psum", bufs=4) as early_psum,
        ):
            sim_sb = {}

            def load_pass(g):
                load_x_rows(0, even_images, nc.sync, new_columns(g))
                load_x_rows(0, odd_images, nc.scalar, new_columns(g))
                sim_sb[g] = early.tile([P, PACK, U], F32, name="sim_sb", tag="stream", bufs=3)
                nc.sync.dma_start(out=sim_sb[g][:], in_=sim_rows[:, z_cols(g), :])

            load_pass(0)
            load_pass(1)
            go_sb = early.tile([P, OX, U], BF16, bufs=1)
            power = early.tile([P, U_TILES, OX, P], F32, bufs=1)

            p_ps = early_psum.tile([P, P], BF16, tag="turn")
            nc.tensor.transpose(p_ps[:], p_rows[:], ident_bf16[:])
            e_col = const.tile([P, U_TILES], F32)
            nc.scalar.activation(out=e_col[:], in_=p_ps[:, 0:U_TILES], func=ACT.Square, scale=1.0 / P_SCALE)
            e_minus_1 = const.tile([P, U_TILES], F32)
            nc.gpsimd.tensor_scalar_add(out=e_minus_1[:], in0=e_col[:], scalar1=-1.0)
            qq_col = const.tile([P, 1], F32)
            nc.scalar.activation(out=qq_col[:], in_=q_col[:], func=ACT.Square, scale=1.0 / Q_SCALE)

            ln_e = const.tile([P, U_TILES], F32)
            nc.scalar.activation(out=ln_e[:], in_=e_col[:], func=ACT.Ln)

            r2_ps = [
                early_psum.tile([P, P], F32, name="r2_ps%d" % ub, bufs=1) for ub in range(U_TILES)
            ]
            w_sb = {}

            def load_w(s):
                w_sb[s] = early.tile(
                    [P, D_TILES_PER_SHIFT, U], BF16, name="w_sb", tag="stream", bufs=3
                )
                nc.sync.dma_start(
                    out=w_sb[s][:], in_=w_tiles[:, s * D_TILES_PER_SHIFT : (s + 1) * D_TILES_PER_SHIFT, :]
                )

            def turn_w(s):
                for ub in range(U_TILES):
                    w_turn = early_psum.tile([P, D_TILES_PER_SHIFT, P], BF16, tag="turn")
                    for t in range(D_TILES_PER_SHIFT):
                        nc.tensor.transpose(w_turn[:, t, :], w_sb[s][:, t, u_cols(ub)], ident_bf16[:])
                    nc.scalar.copy(
                        out=w_t(s)[:, ub].rearrange("p (t d) -> p t d", d=P), in_=w_turn[:]
                    )
                    for t in range(D_TILES_PER_SHIFT):
                        nc.tensor.matmul(
                            out=r2_ps[ub][:],
                            lhsT=w_sb[s][:, t, u_cols(ub)],
                            rhs=w_sb[s][:, t, u_cols(ub)],
                            start=(s == 0 and t == 0),
                            stop=(s == SHIFTS - 1 and t == D_TILES_PER_SHIFT - 1),
                        )

            for g in range(PASSES):
                for ub in range(U_TILES):
                    sim_t = early_psum.tile([P, PACK, P], F32, tag="turn")
                    for t in range(PACK):
                        nc.tensor.transpose(sim_t[:, t, :], sim_sb[g][:, t, u_cols(ub)], ident_f32[:])
                    nc.scalar.activation(out=power[:, ub, z_cols(g), :], in_=sim_t[:], func=ACT.Abs)
                if g + 2 < PASSES:
                    load_pass(g + 2)
                nc.scalar.activation(
                    out=power[:, :, z_cols(g), :], in_=power[:, :, z_cols(g), :], func=ACT.Ln, bias=EPS
                )
            load_w(0)
            nc.sync.dma_start(out=go_sb[:], in_=go_rows)
            shift_x_rows(1)

            first_grouped = {}

            def w_t(s):
                if s < KS:
                    return w_t_first[:, s]
                if not w_t_rest:
                    w_t_rest.append(keep.tile([P, SHIFTS - KS, U_TILES, C], BF16, name="w_t_rest", tag="w_t_rest"))
                return w_t_rest[0][:, s - KS]

            def multiply_first(g):
                multiply_by_rnorm(first_planes[:, g % 2], range(KS), g)

            for s in range(KS):
                new_xn_codes(s)
            multiply_first(0)
            for g in range(PASSES):
                for s in range(KS):
                    first_grouped[s, g] = regroup(first_planes[:, g % 2, :, s, :], nc.vector.tensor_copy)
                if g + 1 < PASSES:
                    multiply_first(g + 1)
                for s in range(KS):
                    quantise(s, g, first_grouped[s, g])

            d_grouped = {}

            def quantise_dsim(g):
                nc.vector.quantize_mx(
                    out=d_codes[:, g, :].bitcast(E5M2_X4),
                    scales=d_scales[:, g, :],
                    in_=d_grouped[g][:].rearrange("p u t -> p (u t)"),
                )

            turn_w(0)
            for g in range(PASSES):
                for ub in range(U_TILES):
                    nc.scalar.activation(
                        out=power[:, ub, z_cols(g), :],
                        in_=power[:, ub, z_cols(g), :],
                        func=ACT.Exp,
                        scale=e_minus_1[:, ub : ub + 1],
                        bias=ln_e[:, ub : ub + 1],
                    )
            for g in range(PASSES):
                d_grouped[g] = xn_pool.tile([P, U, PACK], BF16, name="grouped", align_bytes=64)
                for ub in range(U_TILES):
                    power_rows = early_psum.tile([P, PACK, P], F32, tag="turn")
                    for t in range(PACK):
                        nc.tensor.transpose(power_rows[:, t, :], power[:, ub, g * PACK + t, :], ident_f32[:])
                    nc.vector.tensor_tensor(
                        out=d_grouped[g][:, u_cols(ub), :],
                        in0=power_rows[:].rearrange("p t u -> p u t"),
                        in1=go_sb[:, z_cols(g), u_cols(ub)].rearrange("p t u -> p u t"),
                        op=ALU.mult,
                    )
                if g > 0:
                    quantise_dsim(g - 1)
            quantise_dsim(PASSES - 1)

            for s in range(1, SHIFTS):
                load_w(s)
                turn_w(s)
            new_x_rows(2)
            shift_x_rows(2)

            r2_blocks = const.tile([P, U_TILES, P], F32)
            for ub in range(U_TILES):
                nc.scalar.copy(out=r2_blocks[:, ub, :], in_=r2_ps[ub][:])

        with tc.tile_pool(name="late", bufs=1) as late:
            dws = late.tile([P, U_TILES, D], F32)

            prepare_pair(KS, shared=False)

            r2_col = const.tile([P, U_TILES], F32)
            for ub in range(U_TILES):
                nc.vector.scalar_tensor_tensor(
                    out=r2_blocks[:, ub, :],
                    in0=r2_blocks[:, ub, :],
                    scalar=1.0,
                    in1=ident_f32[:],
                    op0=ALU.mult,
                    op1=ALU.mult,
                    accum_out=r2_col[:, ub : ub + 1],
                )
            nc.gpsimd.tensor_scalar_max(out=r2_col[:], in0=r2_col[:], scalar1=L2_EPS)
            r_col = const.tile([P, U_TILES], F32)
            nc.gpsimd.tensor_tensor(out=r_col[:], in0=r2_col[:], in1=half[:], op=ALU.pow)
            w_norm = const.tile([P, U_TILES], F32)
            nc.gpsimd.tensor_scalar_add(out=w_norm[:], in0=r_col[:], scalar1=qq_col[:, 0:1])
            nc.gpsimd.tensor_tensor(out=a_col[:], in0=w_norm[:], in1=minus_one[:], op=ALU.pow)
            w_norm_r = const.tile([P, U_TILES], F32)
            nc.gpsimd.tensor_tensor(out=w_norm_r[:], in0=w_norm[:], in1=r_col[:], op=ALU.mult)
            nc.gpsimd.tensor_tensor(out=neg_a_over_r[:], in0=w_norm_r[:], in1=minus_one[:], op=ALU.pow)
            nc.gpsimd.tensor_scalar_mul(out=neg_a_over_r[:], in0=neg_a_over_r[:], scalar1=-1.0)

            with tc.psum_pool(name="acc_psum", bufs=8, reuse_waits="tile") as acc_psum:

                def multiply(s):
                    banks = []
                    for ub in range(U_TILES):
                        acc = acc_psum.tile([P, C], F32, name="acc")
                        for g in range(PASSES):
                            nc.tensor.matmul_mx(
                                out=acc[:],
                                lhsT=d_codes[:, g, u_cols(ub)].bitcast(E5M2_X4),
                                lhsT_scale=d_scales[:, g, u_cols(ub)],
                                rhs=xn_codes[s][:, g, :].bitcast(E4M3_X4),
                                rhs_scale=xn_scales[s][:, g, :],
                                start=(g == 0),
                                stop=(g == PASSES - 1),
                            )
                        banks.append(acc)
                    return banks

                banks = {}

                def multiply_shift(s):
                    banks[s] = multiply(s)

                def empty(s):
                    for ub in range(U_TILES):
                        nc.scalar.activation(
                            out=dws[:, ub, d_cols(s)],
                            in_=banks[s][ub][:],
                            func=ACT.Copy,
                            scale=a_col[:, ub : ub + 1],
                        )

                def empty_and_go_on():
                    empty(1)
                    multiply_shift(3)

                multiply_shift(0)
                prepare_single(5)
                empty(0)
                multiply_shift(1)
                multiply_shift(2)
                prepare_pair(6, shared=True, between=empty_and_go_on)
                empty(2)
                multiply_shift(4)
                prepare_single(8)
                for s in range(3, SHIFTS):
                    empty(s)
                    if s + 2 < SHIFTS:
                        multiply_shift(s + 2)

            c_part = const.tile([P, U_TILES, KS], F32)
            for i in range(KS):
                for ub in range(U_TILES):
                    products = code_pool.tile([P, KS * C], F32, name="xn_codes", align_bytes=64)
                    nc.vector.scalar_tensor_tensor(
                        out=products[:].rearrange("p (s d) -> p s d", d=C),
                        in0=dws[:, ub, d_cols(i * KS, KS)].rearrange("p (s d) -> p s d", d=C),
                        scalar=1.0,
                        in1=(w_t_rest[0][:, (i - 1) * KS : i * KS] if i else w_t_first[:])[:, :, ub],
                        op0=ALU.mult,
                        op1=ALU.mult,
                        accum_out=c_part[:, ub, i : i + 1],
                    )

            neg_g = const.tile([P, U_TILES], F32)
            nc.vector.reduce_sum(out=neg_g[:], in_=c_part[:], axis=mybir.AxisListType.X)
            nc.vector.tensor_mul(out=neg_g[:], in0=neg_g[:], in1=neg_a_over_r[:])
            with tc.psum_pool(name="out_psum", bufs=4) as out_psum:
                for s in range(SHIFTS):
                    for ub in range(U_TILES):
                        nc.vector.scalar_tensor_tensor(
                            out=dws[:, ub, d_cols(s)],
                            in0=w_t(s)[:, ub],
                            scalar=neg_g[:, ub : ub + 1],
                            in1=dws[:, ub, d_cols(s)],
                            op0=ALU.mult,
                            op1=ALU.add,
                        )
                    for pair in range(D_TILES_PER_SHIFT // 2):
                        first_tile = s * D_TILES_PER_SHIFT + 2 * pair
                        out_sb = xn_pool.tile([P, 2, U], F32, name="grouped", align_bytes=64)
                        for t in range(2):
                            d_tile = first_tile + t
                            out_ps = out_psum.tile([P, U], F32)
                            for ub in range(U_TILES):
                                nc.tensor.transpose(
                                    out_ps[:, u_cols(ub)], dws[:, ub, d_tile * P : (d_tile + 1) * P], ident_f32[:]
                                )
                            nc.scalar.copy(out=out_sb[:, t, :], in_=out_ps[:])
                        nc.sync.dma_start(out=out_tiles[:, first_tile : first_tile + 2, :], in_=out_sb[:])
